import numpy as np
import ml_dtypes

BF16 = ml_dtypes.bfloat16


def bf(x):
    return np.asarray(x, np.float32).astype(BF16)


def f32(x):
    return np.asarray(x, np.float32)


def f64(x):
    return np.asarray(x).astype(np.float64)


def striped(idx):
    return np.tile(idx.reshape(-1, 16).T, (8, 1))


T, H, S, K, N, R = 128, 2, 2048, 4, 8192, 1024
MU_U, RHO_U = 1.5, 1.0


def setup_inputs():
    x = f32(np.random.standard_normal((T, S)))
    w = f32(np.random.uniform(0.0, 1.0, (H * T, N)) * 2.0 / K)
    idx = np.concatenate([np.random.permutation(S)[:R] for _ in range(N // R)])
    return {"x": x, "w": w, "offs": striped(idx)}


def reference(x, w, offs):
    idx = offs[:16].T.reshape(-1)
    xh = np.tile(f64(x), (H, 1))
    agg = (xh[:, idx] * f64(w)).reshape(H * T, K, S).sum(axis=1)
    return MU_U * (xh - agg) + RHO_U / 2.0 * xh

@@ -1,0 +1,42 @@
+import concourse.mybir as mybir
+
+F32 = mybir.dt.float32
+U16 = mybir.dt.uint16
+MULT = mybir.AluOpType.mult
+ADD = mybir.AluOpType.add
+
+P = 128
+HEADS = 2
+NODES = 2048
+NEIGHBOURS = 4
+OFFS_COLS = NODES // 16
+
+
+def tile_admmblock_kernel(tc, x, w, offs, out):
+    nc = tc.nc
+    with (
+        tc.tile_pool(name="held", bufs=1) as held,
+        tc.tile_pool(name="weights", bufs=4) as weights,
+        tc.tile_pool(name="products", bufs=2) as products,
+        tc.tile_pool(name="results", bufs=2) as results,
+    ):
+        offsets = held.tile([P, NEIGHBOURS * OFFS_COLS], U16, name="offsets")
+        nc.sync.dma_start(offsets[:], offs)
+        signal = held.tile([P, NODES], F32, name="signal")
+        nc.scalar.dma_start(signal[:], x)
+
+        twice = held.tile([P, NODES], F32, name="twice")
+        nc.scalar.mul(twice[:], signal[:], 2.0)
+
+        for h in range(HEADS):
+            rows = slice(h * P, (h + 1) * P)
+            result = results.tile([P, NODES], F32, name="result")
+            for k in range(NEIGHBOURS):
+                edge = weights.tile([P, NODES], F32, name="edge")
+                nc.sync.dma_start(edge[:], w[rows, k * NODES : (k + 1) * NODES])
+                product = products.tile([P, NODES], F32, name="product")
+                picked = signal[:].indirect(offsets[:, k * OFFS_COLS : (k + 1) * OFFS_COLS])
+                nc.vector.tensor_tensor(product[:], picked, edge[:], MULT)
+                so_far = twice if k == 0 else result
+                nc.vector.scalar_tensor_tensor(result[:], product[:], -1.5, so_far[:], MULT, ADD)
+            nc.sync.dma_start(out[rows, :], result[:])

@@ -1,4 +1,5 @@
 import concourse.mybir as mybir
+from concourse.masks import make_identity
 
 F32 = mybir.dt.float32
 U16 = mybir.dt.uint16
@@ -10,26 +11,40 @@ HEADS = 2
 NODES = 2048
 NEIGHBOURS = 4
 OFFS_COLS = NODES // 16
+BANK = 512
+BANKS = NODES // BANK
 
 
 def tile_admmblock_kernel(tc, x, w, offs, out):
     nc = tc.nc
     with (
         tc.tile_pool(name="held", bufs=1) as held,
-        tc.tile_pool(name="weights", bufs=4) as weights,
-        tc.tile_pool(name="products", bufs=2) as products,
+        tc.tile_pool(name="weights", bufs=HEADS * NEIGHBOURS) as weights,
+        tc.tile_pool(name="products", bufs=3) as products,
         tc.tile_pool(name="results", bufs=2) as results,
+        tc.psum_pool(name="sums", bufs=HEADS) as sums,
     ):
         offsets = held.tile([P, NEIGHBOURS * OFFS_COLS], U16, name="offsets")
         nc.sync.dma_start(offsets[:], offs)
         signal = held.tile([P, NODES], F32, name="signal")
         nc.scalar.dma_start(signal[:], x)
 
-        twice = held.tile([P, NODES], F32, name="twice")
-        nc.scalar.mul(twice[:], signal[:], 2.0)
+        identity = held.tile([P, P], F32, name="identity")
+        make_identity(nc, identity[:])
+        plus_two = held.tile([P, P], F32, name="plus_two")
+        nc.scalar.mul(plus_two[:], identity[:], 2.0)
+        minus_three_halves = held.tile([P, P], F32, name="minus_three_halves")
+        nc.scalar.mul(minus_three_halves[:], identity[:], -1.5)
 
         for h in range(HEADS):
             rows = slice(h * P, (h + 1) * P)
+            on_tensor = NEIGHBOURS - 1 if h == HEADS - 1 else NEIGHBOURS
+
+            banks = [sums.tile([P, BANK], F32, name=f"bank{b}") for b in range(BANKS)]
+            for b in range(BANKS):
+                cols = slice(b * BANK, (b + 1) * BANK)
+                nc.tensor.matmul(banks[b][:], plus_two[:], signal[:, cols], start=True, stop=False)
+
             result = results.tile([P, NODES], F32, name="result")
             for k in range(NEIGHBOURS):
                 edge = weights.tile([P, NODES], F32, name="edge")
@@ -37,6 +52,21 @@ def tile_admmblock_kernel(tc, x, w, offs, out):
                 product = products.tile([P, NODES], F32, name="product")
                 picked = signal[:].indirect(offsets[:, k * OFFS_COLS : (k + 1) * OFFS_COLS])
                 nc.vector.tensor_tensor(product[:], picked, edge[:], MULT)
-                so_far = twice if k == 0 else result
-                nc.vector.scalar_tensor_tensor(result[:], product[:], -1.5, so_far[:], MULT, ADD)
+                for b in range(BANKS):
+                    cols = slice(b * BANK, (b + 1) * BANK)
+                    if k < on_tensor:
+                        nc.tensor.matmul(
+                            banks[b][:],
+                            minus_three_halves[:],
+                            product[:, cols],
+                            start=False,
+                            stop=(k == on_tensor - 1),
+                        )
+                    else:
+                        nc.vector.scalar_tensor_tensor(
+                            result[:, cols], product[:, cols], -1.5, banks[b][:], MULT, ADD
+                        )
+            if on_tensor == NEIGHBOURS:
+                for b in range(BANKS):
+                    nc.scalar.copy(result[:, b * BANK : (b + 1) * BANK], banks[b][:])
             nc.sync.dma_start(out[rows, :], result[:])

@@ -66,7 +66,8 @@ def tile_admmblock_kernel(tc, x, w, offs, out):
                         nc.vector.scalar_tensor_tensor(
                             result[:, cols], product[:, cols], -1.5, banks[b][:], MULT, ADD
                         )
-            if on_tensor == NEIGHBOURS:
-                for b in range(BANKS):
-                    nc.scalar.copy(result[:, b * BANK : (b + 1) * BANK], banks[b][:])
-            nc.sync.dma_start(out[rows, :], result[:])
+            for b in range(BANKS):
+                cols = slice(b * BANK, (b + 1) * BANK)
+                if on_tensor == NEIGHBOURS:
+                    nc.scalar.copy(result[:, cols], banks[b][:])
+                nc.sync.dma_start(out[rows, cols], result[:, cols])

@@ -13,6 +13,7 @@ NEIGHBOURS = 4
 OFFS_COLS = NODES // 16
 BANK = 512
 BANKS = NODES // BANK
+WARM_UP = 8
 
 
 def tile_admmblock_kernel(tc, x, w, offs, out):
@@ -41,6 +42,9 @@ def tile_admmblock_kernel(tc, x, w, offs, out):
             on_tensor = NEIGHBOURS - 1 if h == HEADS - 1 else NEIGHBOURS
 
             banks = [sums.tile([P, BANK], F32, name=f"bank{b}") for b in range(BANKS)]
+            if h == 0:
+                for repeat in range(WARM_UP):
+                    nc.tensor.matmul(banks[0][:, :P], identity[:], identity[:], start=True, stop=True)
             for b in range(BANKS):
                 cols = slice(b * BANK, (b + 1) * BANK)
                 nc.tensor.matmul(banks[b][:], plus_two[:], signal[:, cols], start=True, stop=False)

@@ -13,7 +13,8 @@ NEIGHBOURS = 4
 OFFS_COLS = NODES // 16
 BANK = 512
 BANKS = NODES // BANK
-WARM_UP = 8
+FIRST_PIECES = 4
+VECTOR_BANKS = (0, 4)
 
 
 def tile_admmblock_kernel(tc, x, w, offs, out):
@@ -25,10 +26,16 @@ def tile_admmblock_kernel(tc, x, w, offs, out):
         tc.tile_pool(name="results", bufs=2) as results,
         tc.psum_pool(name="sums", bufs=HEADS) as sums,
     ):
+        queues = (nc.sync, nc.scalar)
+
         offsets = held.tile([P, NEIGHBOURS * OFFS_COLS], U16, name="offsets")
         nc.sync.dma_start(offsets[:], offs)
         signal = held.tile([P, NODES], F32, name="signal")
-        nc.scalar.dma_start(signal[:], x)
+        half = NODES // 2
+        for side in range(2):
+            queues[side].dma_start(
+                signal[:, side * half : (side + 1) * half], x[:, side * half : (side + 1) * half]
+            )
 
         identity = held.tile([P, P], F32, name="identity")
         make_identity(nc, identity[:])
@@ -39,12 +46,7 @@ def tile_admmblock_kernel(tc, x, w, offs, out):
 
         for h in range(HEADS):
             rows = slice(h * P, (h + 1) * P)
-            on_tensor = NEIGHBOURS - 1 if h == HEADS - 1 else NEIGHBOURS
-
             banks = [sums.tile([P, BANK], F32, name=f"bank{b}") for b in range(BANKS)]
-            if h == 0:
-                for repeat in range(WARM_UP):
-                    nc.tensor.matmul(banks[0][:, :P], identity[:], identity[:], start=True, stop=True)
             for b in range(BANKS):
                 cols = slice(b * BANK, (b + 1) * BANK)
                 nc.tensor.matmul(banks[b][:], plus_two[:], signal[:, cols], start=True, stop=False)
@@ -52,26 +54,33 @@ def tile_admmblock_kernel(tc, x, w, offs, out):
             result = results.tile([P, NODES], F32, name="result")
             for k in range(NEIGHBOURS):
                 edge = weights.tile([P, NODES], F32, name="edge")
-                nc.sync.dma_start(edge[:], w[rows, k * NODES : (k + 1) * NODES])
                 product = products.tile([P, NODES], F32, name="product")
-                picked = signal[:].indirect(offsets[:, k * OFFS_COLS : (k + 1) * OFFS_COLS])
-                nc.vector.tensor_tensor(product[:], picked, edge[:], MULT)
+                pieces = FIRST_PIECES if h == 0 and k == 0 else 1
+                width = NODES // pieces
+                for piece in range(pieces):
+                    cols = slice(piece * width, (piece + 1) * width)
+                    entry = k * NODES + piece * width
+                    queues[(k + piece) % 2].dma_start(edge[:, cols], w[rows, entry : entry + width])
+                    picked = signal[:].indirect(offsets[:, entry // 16 : (entry + width) // 16])
+                    nc.vector.tensor_tensor(product[:, cols], picked, edge[:, cols], MULT)
+
                 for b in range(BANKS):
                     cols = slice(b * BANK, (b + 1) * BANK)
-                    if k < on_tensor:
+                    by_vector = b >= BANKS - VECTOR_BANKS[h]
+                    last_on_tensor = NEIGHBOURS - 2 if by_vector else NEIGHBOURS - 1
+                    if k <= last_on_tensor:
                         nc.tensor.matmul(
                             banks[b][:],
                             minus_three_halves[:],
                             product[:, cols],
                             start=False,
-                            stop=(k == on_tensor - 1),
+                            stop=(k == last_on_tensor),
                         )
                     else:
                         nc.vector.scalar_tensor_tensor(
                             result[:, cols], product[:, cols], -1.5, banks[b][:], MULT, ADD
                         )
-            for b in range(BANKS):
-                cols = slice(b * BANK, (b + 1) * BANK)
-                if on_tensor == NEIGHBOURS:
-                    nc.scalar.copy(result[:, cols], banks[b][:])
-                nc.sync.dma_start(out[rows, cols], result[:, cols])
+                    if k == NEIGHBOURS - 1:
+                        if not by_vector:
+                            nc.scalar.copy(result[:, cols], banks[b][:])
+                        nc.sync.dma_start(out[rows, cols], result[:, cols])

@@ -1,10 +1,10 @@
 import concourse.mybir as mybir
-from concourse.masks import make_identity
 
 F32 = mybir.dt.float32
 U16 = mybir.dt.uint16
 MULT = mybir.AluOpType.mult
 ADD = mybir.AluOpType.add
+NOT_EQUAL = mybir.AluOpType.not_equal
 
 P = 128
 HEADS = 2
@@ -14,7 +14,20 @@ OFFS_COLS = NODES // 16
 BANK = 512
 BANKS = NODES // BANK
 FIRST_PIECES = 4
-VECTOR_BANKS = (0, 4)
+VECTOR_BANKS = (2, 4)
+
+
+def scaled_identity(nc, diagonal, scale):
+    nc.gpsimd.memset(diagonal, 0.0)
+    nc.gpsimd.affine_select(
+        out=diagonal,
+        in_=diagonal,
+        pattern=[[-1, P]],
+        compare_op=NOT_EQUAL,
+        fill=scale,
+        base=0,
+        channel_multiplier=1,
+    )
 
 
 def tile_admmblock_kernel(tc, x, w, offs, out):
@@ -22,7 +35,7 @@ def tile_admmblock_kernel(tc, x, w, offs, out):
     with (
         tc.tile_pool(name="held", bufs=1) as held,
         tc.tile_pool(name="weights", bufs=HEADS * NEIGHBOURS) as weights,
-        tc.tile_pool(name="products", bufs=3) as products,
+        tc.tile_pool(name="products", bufs=4) as products,
         tc.tile_pool(name="results", bufs=2) as results,
         tc.psum_pool(name="sums", bufs=HEADS) as sums,
     ):
@@ -37,12 +50,10 @@ def tile_admmblock_kernel(tc, x, w, offs, out):
                 signal[:, side * half : (side + 1) * half], x[:, side * half : (side + 1) * half]
             )
 
-        identity = held.tile([P, P], F32, name="identity")
-        make_identity(nc, identity[:])
         plus_two = held.tile([P, P], F32, name="plus_two")
-        nc.scalar.mul(plus_two[:], identity[:], 2.0)
+        scaled_identity(nc, plus_two[:], 2.0)
         minus_three_halves = held.tile([P, P], F32, name="minus_three_halves")
-        nc.scalar.mul(minus_three_halves[:], identity[:], -1.5)
+        scaled_identity(nc, minus_three_halves[:], -1.5)
 
         for h in range(HEADS):
             rows = slice(h * P, (h + 1) * P)
@@ -60,7 +71,7 @@ def tile_admmblock_kernel(tc, x, w, offs, out):
                 for piece in range(pieces):
                     cols = slice(piece * width, (piece + 1) * width)
                     entry = k * NODES + piece * width
-                    queues[(k + piece) % 2].dma_start(edge[:, cols], w[rows, entry : entry + width])
+                    queues[(k + piece + 1) % 2].dma_start(edge[:, cols], w[rows, entry : entry + width])
                     picked = signal[:].indirect(offsets[:, entry // 16 : (entry + width) // 16])
                     nc.vector.tensor_tensor(product[:, cols], picked, edge[:, cols], MULT)
 

@@ -14,7 +14,7 @@ OFFS_COLS = NODES // 16
 BANK = 512
 BANKS = NODES // BANK
 FIRST_PIECES = 4
-VECTOR_BANKS = (2, 4)
+VECTOR_BANKS = (0, 4)
 
 
 def scaled_identity(nc, diagonal, scale):

@@ -14,7 +14,7 @@ OFFS_COLS = NODES // 16
 BANK = 512
 BANKS = NODES // BANK
 FIRST_PIECES = 4
-VECTOR_BANKS = (0, 4)
+VECTOR_BANKS = (1, 4)
 
 
 def scaled_identity(nc, diagonal, scale):
@@ -77,7 +77,7 @@ def tile_admmblock_kernel(tc, x, w, offs, out):
 
                 for b in range(BANKS):
                     cols = slice(b * BANK, (b + 1) * BANK)
-                    by_vector = b >= BANKS - VECTOR_BANKS[h]
+                    by_vector = b < VECTOR_BANKS[h]
                     last_on_tensor = NEIGHBOURS - 2 if by_vector else NEIGHBOURS - 1
                     if k <= last_on_tensor:
                         nc.tensor.matmul(

@@ -13,8 +13,8 @@ NEIGHBOURS = 4
 OFFS_COLS = NODES // 16
 BANK = 512
 BANKS = NODES // BANK
-FIRST_PIECES = 4
-VECTOR_BANKS = (1, 4)
+END_PIECES = BANKS
+VECTOR_BANKS = (0, 4)
 
 
 def scaled_identity(nc, diagonal, scale):
@@ -35,38 +35,44 @@ def tile_admmblock_kernel(tc, x, w, offs, out):
     with (
         tc.tile_pool(name="held", bufs=1) as held,
         tc.tile_pool(name="weights", bufs=HEADS * NEIGHBOURS) as weights,
-        tc.tile_pool(name="products", bufs=4) as products,
+        tc.tile_pool(name="products", bufs=6) as products,
         tc.tile_pool(name="results", bufs=2) as results,
-        tc.psum_pool(name="sums", bufs=HEADS) as sums,
+        tc.psum_pool(name="sums", bufs=1) as sums,
     ):
         queues = (nc.sync, nc.scalar)
 
+        signal = held.tile([P, NODES], F32, name="signal")
+        for b in range(BANKS):
+            cols = slice(b * BANK, (b + 1) * BANK)
+            queues[b % 2].dma_start(signal[:, cols], x[:, cols])
         offsets = held.tile([P, NEIGHBOURS * OFFS_COLS], U16, name="offsets")
         nc.sync.dma_start(offsets[:], offs)
-        signal = held.tile([P, NODES], F32, name="signal")
-        half = NODES // 2
-        for side in range(2):
-            queues[side].dma_start(
-                signal[:, side * half : (side + 1) * half], x[:, side * half : (side + 1) * half]
-            )
 
         plus_two = held.tile([P, P], F32, name="plus_two")
         scaled_identity(nc, plus_two[:], 2.0)
         minus_three_halves = held.tile([P, P], F32, name="minus_three_halves")
         scaled_identity(nc, minus_three_halves[:], -1.5)
 
+        sums_of = [
+            [sums.tile([P, BANK], F32, name=f"head{h}_bank{b}") for b in range(BANKS)] for h in range(HEADS)
+        ]
+        for b in range(BANKS):
+            cols = slice(b * BANK, (b + 1) * BANK)
+            for h in range(HEADS):
+                nc.tensor.matmul(sums_of[h][b][:], plus_two[:], signal[:, cols], start=True, stop=False)
+
+        postponed = []
+
         for h in range(HEADS):
             rows = slice(h * P, (h + 1) * P)
-            banks = [sums.tile([P, BANK], F32, name=f"bank{b}") for b in range(BANKS)]
-            for b in range(BANKS):
-                cols = slice(b * BANK, (b + 1) * BANK)
-                nc.tensor.matmul(banks[b][:], plus_two[:], signal[:, cols], start=True, stop=False)
-
+            banks = sums_of[h]
             result = results.tile([P, NODES], F32, name="result")
             for k in range(NEIGHBOURS):
                 edge = weights.tile([P, NODES], F32, name="edge")
                 product = products.tile([P, NODES], F32, name="product")
-                pieces = FIRST_PIECES if h == 0 and k == 0 else 1
+                first = h == 0 and k == 0
+                last = h == HEADS - 1 and k == NEIGHBOURS - 1
+                pieces = END_PIECES if first or last else 1
                 width = NODES // pieces
                 for piece in range(pieces):
                     cols = slice(piece * width, (piece + 1) * width)
@@ -74,6 +80,18 @@ def tile_admmblock_kernel(tc, x, w, offs, out):
                     queues[(k + piece + 1) % 2].dma_start(edge[:, cols], w[rows, entry : entry + width])
                     picked = signal[:].indirect(offsets[:, entry // 16 : (entry + width) // 16])
                     nc.vector.tensor_tensor(product[:, cols], picked, edge[:, cols], MULT)
+                    if last:
+                        nc.vector.scalar_tensor_tensor(
+                            result[:, cols], product[:, cols], -1.5, banks[piece][:], MULT, ADD
+                        )
+                        nc.sync.dma_start(out[rows, cols], result[:, cols])
+
+                for earlier_result, earlier_product, earlier_bank, earlier_rows, cols in postponed:
+                    nc.vector.scalar_tensor_tensor(
+                        earlier_result[:, cols], earlier_product[:, cols], -1.5, earlier_bank[:], MULT, ADD
+                    )
+                    nc.sync.dma_start(out[earlier_rows, cols], earlier_result[:, cols])
+                postponed = []
 
                 for b in range(BANKS):
                     cols = slice(b * BANK, (b + 1) * BANK)
@@ -87,11 +105,8 @@ def tile_admmblock_kernel(tc, x, w, offs, out):
                             start=False,
                             stop=(k == last_on_tensor),
                         )
-                    else:
-                        nc.vector.scalar_tensor_tensor(
-                            result[:, cols], product[:, cols], -1.5, banks[b][:], MULT, ADD
-                        )
-                    if k == NEIGHBOURS - 1:
-                        if not by_vector:
-                            nc.scalar.copy(result[:, cols], banks[b][:])
+                    elif h < HEADS - 1:
+                        postponed.append((result, product, banks[b], rows, cols))
+                    if k == NEIGHBOURS - 1 and not by_vector:
+                        nc.scalar.copy(result[:, cols], banks[b][:])
                         nc.sync.dma_start(out[rows, cols], result[:, cols])

@@ -10,11 +10,9 @@ P = 128
 HEADS = 2
 NODES = 2048
 NEIGHBOURS = 4
-OFFS_COLS = NODES // 16
 BANK = 512
 BANKS = NODES // BANK
-END_PIECES = BANKS
-VECTOR_BANKS = (0, 4)
+FIRST_WIDTH = 128
 
 
 def scaled_identity(nc, diagonal, scale):
@@ -30,22 +28,27 @@ def scaled_identity(nc, diagonal, scale):
     )
 
 
+def doubling_widths(first, total):
+    widths = [first]
+    while sum(widths) < total:
+        widths.append(sum(widths))
+    return widths
+
+
 def tile_admmblock_kernel(tc, x, w, offs, out):
     nc = tc.nc
     with (
         tc.tile_pool(name="held", bufs=1) as held,
         tc.tile_pool(name="weights", bufs=HEADS * NEIGHBOURS) as weights,
         tc.tile_pool(name="products", bufs=6) as products,
-        tc.tile_pool(name="results", bufs=2) as results,
+        tc.tile_pool(name="results", bufs=HEADS) as results,
         tc.psum_pool(name="sums", bufs=1) as sums,
     ):
-        queues = (nc.sync, nc.scalar)
-
         signal = held.tile([P, NODES], F32, name="signal")
         for b in range(BANKS):
             cols = slice(b * BANK, (b + 1) * BANK)
-            queues[b % 2].dma_start(signal[:, cols], x[:, cols])
-        offsets = held.tile([P, NEIGHBOURS * OFFS_COLS], U16, name="offsets")
+            nc.sync.dma_start(signal[:, cols], x[:, cols])
+        offsets = held.tile([P, NEIGHBOURS * NODES // 16], U16, name="offsets")
         nc.sync.dma_start(offsets[:], offs)
 
         plus_two = held.tile([P, P], F32, name="plus_two")
@@ -61,52 +64,50 @@ def tile_admmblock_kernel(tc, x, w, offs, out):
             for h in range(HEADS):
                 nc.tensor.matmul(sums_of[h][b][:], plus_two[:], signal[:, cols], start=True, stop=False)
 
-        postponed = []
-
         for h in range(HEADS):
             rows = slice(h * P, (h + 1) * P)
-            banks = sums_of[h]
             result = results.tile([P, NODES], F32, name="result")
             for k in range(NEIGHBOURS):
+                very_first = h == 0 and k == 0
+                very_last = h == HEADS - 1 and k == NEIGHBOURS - 1
                 edge = weights.tile([P, NODES], F32, name="edge")
                 product = products.tile([P, NODES], F32, name="product")
-                first = h == 0 and k == 0
-                last = h == HEADS - 1 and k == NEIGHBOURS - 1
-                pieces = END_PIECES if first or last else 1
-                width = NODES // pieces
-                for piece in range(pieces):
-                    cols = slice(piece * width, (piece + 1) * width)
-                    entry = k * NODES + piece * width
-                    queues[(k + piece + 1) % 2].dma_start(edge[:, cols], w[rows, entry : entry + width])
+
+                if very_first:
+                    widths = doubling_widths(FIRST_WIDTH, NODES)
+                elif very_last:
+                    widths = [BANK] * (BANKS - 1) + [BANK // 2] * 2
+                else:
+                    widths = [NODES]
+                loads = widths if very_first else [NODES]
+
+                start = 0
+                for width in loads:
+                    entry = k * NODES + start
+                    nc.sync.dma_start(edge[:, start : start + width], w[rows, entry : entry + width])
+                    start += width
+
+                start = 0
+                for width in widths:
+                    cols = slice(start, start + width)
+                    entry = k * NODES + start
                     picked = signal[:].indirect(offsets[:, entry // 16 : (entry + width) // 16])
                     nc.vector.tensor_tensor(product[:, cols], picked, edge[:, cols], MULT)
-                    if last:
+                    if very_last:
+                        in_bank = slice(start % BANK, start % BANK + width)
                         nc.vector.scalar_tensor_tensor(
-                            result[:, cols], product[:, cols], -1.5, banks[piece][:], MULT, ADD
+                            result[:, cols], product[:, cols], -1.5, sums_of[h][start // BANK][:, in_bank], MULT, ADD
                         )
                         nc.sync.dma_start(out[rows, cols], result[:, cols])
+                    start += width
 
-                for earlier_result, earlier_product, earlier_bank, earlier_rows, cols in postponed:
-                    nc.vector.scalar_tensor_tensor(
-                        earlier_result[:, cols], earlier_product[:, cols], -1.5, earlier_bank[:], MULT, ADD
-                    )
-                    nc.sync.dma_start(out[earlier_rows, cols], earlier_result[:, cols])
-                postponed = []
-
-                for b in range(BANKS):
-                    cols = slice(b * BANK, (b + 1) * BANK)
-                    by_vector = b < VECTOR_BANKS[h]
-                    last_on_tensor = NEIGHBOURS - 2 if by_vector else NEIGHBOURS - 1
-                    if k <= last_on_tensor:
+                if not very_last:
+                    closing = k == NEIGHBOURS - 1 or (h == HEADS - 1 and k == NEIGHBOURS - 2)
+                    for b in range(BANKS):
+                        cols = slice(b * BANK, (b + 1) * BANK)
                         nc.tensor.matmul(
-                            banks[b][:],
-                            minus_three_halves[:],
-                            product[:, cols],
-                            start=False,
-                            stop=(k == last_on_tensor),
+                            sums_of[h][b][:], minus_three_halves[:], product[:, cols], start=False, stop=closing
                         )
-                    elif h < HEADS - 1:
-                        postponed.append((result, product, banks[b], rows, cols))
-                    if k == NEIGHBOURS - 1 and not by_vector:
-                        nc.scalar.copy(result[:, cols], banks[b][:])
-                        nc.sync.dma_start(out[rows, cols], result[:, cols])
+                        if k == NEIGHBOURS - 1:
+                            nc.scalar.copy(result[:, cols], sums_of[h][b][:])
+                            nc.sync.dma_start(out[rows, cols], result[:, cols])

@@ -28,10 +28,10 @@ def scaled_identity(nc, diagonal, scale):
     )
 
 
-def doubling_widths(first, total):
+def growing_widths(first, most, total):
     widths = [first]
     while sum(widths) < total:
-        widths.append(sum(widths))
+        widths.append(min(sum(widths), most))
     return widths
 
 
@@ -44,10 +44,12 @@ def tile_admmblock_kernel(tc, x, w, offs, out):
         tc.tile_pool(name="results", bufs=HEADS) as results,
         tc.psum_pool(name="sums", bufs=1) as sums,
     ):
+        start_widths = growing_widths(FIRST_WIDTH, BANK, NODES)
         signal = held.tile([P, NODES], F32, name="signal")
-        for b in range(BANKS):
-            cols = slice(b * BANK, (b + 1) * BANK)
-            nc.sync.dma_start(signal[:, cols], x[:, cols])
+        start = 0
+        for width in start_widths:
+            nc.sync.dma_start(signal[:, start : start + width], x[:, start : start + width])
+            start += width
         offsets = held.tile([P, NEIGHBOURS * NODES // 16], U16, name="offsets")
         nc.sync.dma_start(offsets[:], offs)
 
@@ -59,10 +61,18 @@ def tile_admmblock_kernel(tc, x, w, offs, out):
         sums_of = [
             [sums.tile([P, BANK], F32, name=f"head{h}_bank{b}") for b in range(BANKS)] for h in range(HEADS)
         ]
-        for b in range(BANKS):
-            cols = slice(b * BANK, (b + 1) * BANK)
+        start = 0
+        for width in start_widths:
+            in_bank = slice(start % BANK, start % BANK + width)
             for h in range(HEADS):
-                nc.tensor.matmul(sums_of[h][b][:], plus_two[:], signal[:, cols], start=True, stop=False)
+                nc.tensor.matmul(
+                    sums_of[h][start // BANK][:, in_bank],
+                    plus_two[:],
+                    signal[:, start : start + width],
+                    start=(start % BANK == 0),
+                    stop=False,
+                )
+            start += width
 
         for h in range(HEADS):
             rows = slice(h * P, (h + 1) * P)
@@ -74,7 +84,7 @@ def tile_admmblock_kernel(tc, x, w, offs, out):
                 product = products.tile([P, NODES], F32, name="product")
 
                 if very_first:
-                    widths = doubling_widths(FIRST_WIDTH, NODES)
+                    widths = start_widths
                 elif very_last:
                     widths = [BANK] * (BANKS - 1) + [BANK // 2] * 2
                 else:

@@ -11,8 +11,8 @@ HEADS = 2
 NODES = 2048
 NEIGHBOURS = 4
 BANK = 512
-BANKS = NODES // BANK
-FIRST_WIDTH = 128
+GROUP_WIDTHS = ((BANK, BANK, BANK, BANK), (BANK, BANK, BANK, BANK // 2, BANK // 2))
+START_WIDTHS = (128, 128, 256, BANK, BANK, BANK // 2, BANK // 2)
 
 
 def scaled_identity(nc, diagonal, scale):
@@ -28,11 +28,8 @@ def scaled_identity(nc, diagonal, scale):
     )
 
 
-def growing_widths(first, most, total):
-    widths = [first]
-    while sum(widths) < total:
-        widths.append(min(sum(widths), most))
-    return widths
+def spans(widths):
+    return [(sum(widths[:i]), width) for i, width in enumerate(widths)]
 
 
 def tile_admmblock_kernel(tc, x, w, offs, out):
@@ -44,12 +41,9 @@ def tile_admmblock_kernel(tc, x, w, offs, out):
         tc.tile_pool(name="results", bufs=HEADS) as results,
         tc.psum_pool(name="sums", bufs=1) as sums,
     ):
-        start_widths = growing_widths(FIRST_WIDTH, BANK, NODES)
         signal = held.tile([P, NODES], F32, name="signal")
-        start = 0
-        for width in start_widths:
+        for start, width in spans(START_WIDTHS):
             nc.sync.dma_start(signal[:, start : start + width], x[:, start : start + width])
-            start += width
         offsets = held.tile([P, NEIGHBOURS * NODES // 16], U16, name="offsets")
         nc.sync.dma_start(offsets[:], offs)
 
@@ -58,25 +52,36 @@ def tile_admmblock_kernel(tc, x, w, offs, out):
         minus_three_halves = held.tile([P, P], F32, name="minus_three_halves")
         scaled_identity(nc, minus_three_halves[:], -1.5)
 
-        sums_of = [
-            [sums.tile([P, BANK], F32, name=f"head{h}_bank{b}") for b in range(BANKS)] for h in range(HEADS)
-        ]
-        start = 0
-        for width in start_widths:
-            in_bank = slice(start % BANK, start % BANK + width)
+        groups = [spans(GROUP_WIDTHS[h]) for h in range(HEADS)]
+        late_group = (HEADS - 1, groups[HEADS - 1][-1][0])
+        bank_of = {}
+
+        def add_two_x(h, start, width):
+            first = max(group_start for group_start, group_width in groups[h] if group_start <= start)
+            nc.tensor.matmul(
+                bank_of[h, first][:, start - first : start - first + width],
+                plus_two[:],
+                signal[:, start : start + width],
+                start=(start == first),
+                stop=False,
+            )
+
+        for h in range(HEADS):
+            for start, width in groups[h]:
+                if (h, start) != late_group:
+                    bank_of[h, start] = sums.tile([P, BANK], F32, name=f"head{h}_from{start}")
+        for start, width in spans(START_WIDTHS):
             for h in range(HEADS):
-                nc.tensor.matmul(
-                    sums_of[h][start // BANK][:, in_bank],
-                    plus_two[:],
-                    signal[:, start : start + width],
-                    start=(start % BANK == 0),
-                    stop=False,
-                )
-            start += width
+                if (h, start) != late_group:
+                    add_two_x(h, start, width)
 
         for h in range(HEADS):
             rows = slice(h * P, (h + 1) * P)
             result = results.tile([P, NODES], F32, name="result")
+            if h == late_group[0]:
+                bank_of[late_group] = sums.tile([P, BANK], F32, name="late_sum", tag="head0_from0")
+                add_two_x(h, late_group[1], groups[h][-1][1])
+
             for k in range(NEIGHBOURS):
                 very_first = h == 0 and k == 0
                 very_last = h == HEADS - 1 and k == NEIGHBOURS - 1
@@ -84,40 +89,34 @@ def tile_admmblock_kernel(tc, x, w, offs, out):
                 product = products.tile([P, NODES], F32, name="product")
 
                 if very_first:
-                    widths = start_widths
+                    pieces = spans(START_WIDTHS)
                 elif very_last:
-                    widths = [BANK] * (BANKS - 1) + [BANK // 2] * 2
+                    pieces = groups[h]
                 else:
-                    widths = [NODES]
-                loads = widths if very_first else [NODES]
+                    pieces = [(0, NODES)]
 
-                start = 0
-                for width in loads:
+                for start, width in pieces if very_first else [(0, NODES)]:
                     entry = k * NODES + start
                     nc.sync.dma_start(edge[:, start : start + width], w[rows, entry : entry + width])
-                    start += width
 
-                start = 0
-                for width in widths:
+                for start, width in pieces:
                     cols = slice(start, start + width)
                     entry = k * NODES + start
                     picked = signal[:].indirect(offsets[:, entry // 16 : (entry + width) // 16])
                     nc.vector.tensor_tensor(product[:, cols], picked, edge[:, cols], MULT)
                     if very_last:
-                        in_bank = slice(start % BANK, start % BANK + width)
                         nc.vector.scalar_tensor_tensor(
-                            result[:, cols], product[:, cols], -1.5, sums_of[h][start // BANK][:, in_bank], MULT, ADD
+                            result[:, cols], product[:, cols], -1.5, bank_of[h, start][:, :width], MULT, ADD
                         )
                         nc.sync.dma_start(out[rows, cols], result[:, cols])
-                    start += width
 
                 if not very_last:
                     closing = k == NEIGHBOURS - 1 or (h == HEADS - 1 and k == NEIGHBOURS - 2)
-                    for b in range(BANKS):
-                        cols = slice(b * BANK, (b + 1) * BANK)
+                    for start, width in groups[h]:
+                        cols = slice(start, start + width)
                         nc.tensor.matmul(
-                            sums_of[h][b][:], minus_three_halves[:], product[:, cols], start=False, stop=closing
+                            bank_of[h, start][:, :width], minus_three_halves[:], product[:, cols], start=False, stop=closing
                         )
                         if k == NEIGHBOURS - 1:
-                            nc.scalar.copy(result[:, cols], sums_of[h][b][:])
+                            nc.scalar.copy(result[:, cols], bank_of[h, start][:, :width])
                             nc.sync.dma_start(out[rows, cols], result[:, cols])

@@ -12,7 +12,8 @@ NODES = 2048
 NEIGHBOURS = 4
 BANK = 512
 GROUP_WIDTHS = ((BANK, BANK, BANK, BANK), (BANK, BANK, BANK, BANK // 2, BANK // 2))
-START_WIDTHS = (128, 128, 256, BANK, BANK, BANK // 2, BANK // 2)
+SIGNAL_WIDTHS = (BANK, BANK, 2 * BANK)
+FIRST_EDGE_WIDTHS = (128, 256, 512, 1152)
 
 
 def scaled_identity(nc, diagonal, scale):
@@ -42,7 +43,7 @@ def tile_admmblock_kernel(tc, x, w, offs, out):
         tc.psum_pool(name="sums", bufs=1) as sums,
     ):
         signal = held.tile([P, NODES], F32, name="signal")
-        for start, width in spans(START_WIDTHS):
+        for start, width in spans(SIGNAL_WIDTHS):
             nc.sync.dma_start(signal[:, start : start + width], x[:, start : start + width])
         offsets = held.tile([P, NEIGHBOURS * NODES // 16], U16, name="offsets")
         nc.sync.dma_start(offsets[:], offs)
@@ -56,31 +57,23 @@ def tile_admmblock_kernel(tc, x, w, offs, out):
         late_group = (HEADS - 1, groups[HEADS - 1][-1][0])
         bank_of = {}
 
-        def add_two_x(h, start, width):
-            first = max(group_start for group_start, group_width in groups[h] if group_start <= start)
+        def open_sum(h, start, width):
             nc.tensor.matmul(
-                bank_of[h, first][:, start - first : start - first + width],
-                plus_two[:],
-                signal[:, start : start + width],
-                start=(start == first),
-                stop=False,
+                bank_of[h, start][:, :width], plus_two[:], signal[:, start : start + width], start=True, stop=False
             )
 
-        for h in range(HEADS):
-            for start, width in groups[h]:
-                if (h, start) != late_group:
-                    bank_of[h, start] = sums.tile([P, BANK], F32, name=f"head{h}_from{start}")
-        for start, width in spans(START_WIDTHS):
-            for h in range(HEADS):
-                if (h, start) != late_group:
-                    add_two_x(h, start, width)
+        early_groups = [(start, h, width) for h in range(HEADS) for start, width in groups[h] if (h, start) != late_group]
+        for start, h, width in early_groups:
+            bank_of[h, start] = sums.tile([P, BANK], F32, name=f"head{h}_from{start}")
+        for start, h, width in sorted(early_groups):
+            open_sum(h, start, width)
 
         for h in range(HEADS):
             rows = slice(h * P, (h + 1) * P)
             result = results.tile([P, NODES], F32, name="result")
             if h == late_group[0]:
                 bank_of[late_group] = sums.tile([P, BANK], F32, name="late_sum", tag="head0_from0")
-                add_two_x(h, late_group[1], groups[h][-1][1])
+                open_sum(h, late_group[1], groups[h][-1][1])
 
             for k in range(NEIGHBOURS):
                 very_first = h == 0 and k == 0
@@ -89,7 +82,7 @@ def tile_admmblock_kernel(tc, x, w, offs, out):
                 product = products.tile([P, NODES], F32, name="product")
 
                 if very_first:
-                    pieces = spans(START_WIDTHS)
+                    pieces = spans(FIRST_EDGE_WIDTHS)
                 elif very_last:
                     pieces = groups[h]
                 else:

import concourse.mybir as mybir

F32 = mybir.dt.float32
U16 = mybir.dt.uint16
MULT = mybir.AluOpType.mult
ADD = mybir.AluOpType.add
NOT_EQUAL = mybir.AluOpType.not_equal

P = 128
HEADS = 2
NODES = 2048
NEIGHBOURS = 4
BANK = 512
GROUP_WIDTHS = ((BANK, BANK, BANK, BANK), (BANK, BANK, BANK, BANK // 2, BANK // 2))
SIGNAL_WIDTHS = (BANK, BANK, 2 * BANK)
FIRST_EDGE_WIDTHS = (128, 256, 512, 1152)


def scaled_identity(nc, diagonal, scale):
    nc.gpsimd.memset(diagonal, 0.0)
    nc.gpsimd.affine_select(
        out=diagonal,
        in_=diagonal,
        pattern=[[-1, P]],
        compare_op=NOT_EQUAL,
        fill=scale,
        base=0,
        channel_multiplier=1,
    )


def spans(widths):
    return [(sum(widths[:i]), width) for i, width in enumerate(widths)]


def tile_admmblock_kernel(tc, x, w, offs, out):
    nc = tc.nc
    with (
        tc.tile_pool(name="held", bufs=1) as held,
        tc.tile_pool(name="weights", bufs=HEADS * NEIGHBOURS) as weights,
        tc.tile_pool(name="products", bufs=6) as products,
        tc.tile_pool(name="results", bufs=HEADS) as results,
        tc.psum_pool(name="sums", bufs=1) as sums,
    ):
        signal = held.tile([P, NODES], F32, name="signal")
        for start, width in spans(SIGNAL_WIDTHS):
            nc.sync.dma_start(signal[:, start : start + width], x[:, start : start + width])
        offsets = held.tile([P, NEIGHBOURS * NODES // 16], U16, name="offsets")
        nc.sync.dma_start(offsets[:], offs)

        plus_two = held.tile([P, P], F32, name="plus_two")
        scaled_identity(nc, plus_two[:], 2.0)
        minus_three_halves = held.tile([P, P], F32, name="minus_three_halves")
        scaled_identity(nc, minus_three_halves[:], -1.5)

        groups = [spans(GROUP_WIDTHS[h]) for h in range(HEADS)]
        late_group = (HEADS - 1, groups[HEADS - 1][-1][0])
        bank_of = {}

        def open_sum(h, start, width):
            nc.tensor.matmul(
                bank_of[h, start][:, :width], plus_two[:], signal[:, start : start + width], start=True, stop=False
            )

        early_groups = [(start, h, width) for h in range(HEADS) for start, width in groups[h] if (h, start) != late_group]
        for start, h, width in early_groups:
            bank_of[h, start] = sums.tile([P, BANK], F32, name=f"head{h}_from{start}")
        for start, h, width in sorted(early_groups):
            open_sum(h, start, width)

        for h in range(HEADS):
            rows = slice(h * P, (h + 1) * P)
            result = results.tile([P, NODES], F32, name="result")
            if h == late_group[0]:
                bank_of[late_group] = sums.tile([P, BANK], F32, name="late_sum", tag="head0_from0")
                open_sum(h, late_group[1], groups[h][-1][1])

            for k in range(NEIGHBOURS):
                very_first = h == 0 and k == 0
                very_last = h == HEADS - 1 and k == NEIGHBOURS - 1
                edge = weights.tile([P, NODES], F32, name="edge")
                product = products.tile([P, NODES], F32, name="product")

                if very_first:
                    pieces = spans(FIRST_EDGE_WIDTHS)
                elif very_last:
                    pieces = groups[h]
                else:
                    pieces = [(0, NODES)]

                for start, width in pieces if very_first else [(0, NODES)]:
                    entry = k * NODES + start
                    nc.sync.dma_start(edge[:, start : start + width], w[rows, entry : entry + width])

                for start, width in pieces:
                    cols = slice(start, start + width)
                    entry = k * NODES + start
                    picked = signal[:].indirect(offsets[:, entry // 16 : (entry + width) // 16])
                    nc.vector.tensor_tensor(product[:, cols], picked, edge[:, cols], MULT)
                    if very_last:
                        nc.vector.scalar_tensor_tensor(
                            result[:, cols], product[:, cols], -1.5, bank_of[h, start][:, :width], MULT, ADD
                        )
                        nc.sync.dma_start(out[rows, cols], result[:, cols])

                if not very_last:
                    closing = k == NEIGHBOURS - 1 or (h == HEADS - 1 and k == NEIGHBOURS - 2)
                    for start, width in groups[h]:
                        cols = slice(start, start + width)
                        nc.tensor.matmul(
                            bank_of[h, start][:, :width], minus_three_halves[:], product[:, cols], start=False, stop=closing
                        )
                        if k == NEIGHBOURS - 1:
                            nc.scalar.copy(result[:, cols], bank_of[h, start][:, :width])
                            nc.sync.dma_start(out[rows, cols], result[:, cols])
